import numpy as np
import ml_dtypes


def mxq(x, axis, fmt="e4m3"):
    dtype, down = {"e4m3": (ml_dtypes.float8_e4m3fn, 7), "e5m2": (ml_dtypes.float8_e5m2, 14)}[fmt]
    v = np.moveaxis(np.asarray(x, np.float32).astype(ml_dtypes.bfloat16).astype(np.float64), axis, -1)
    blocks = v.reshape(v.shape[:-1] + (-1, 32))
    amax = np.abs(blocks).max(-1, keepdims=True)
    byte = np.maximum(np.where(amax > 0, np.frexp(amax)[1] - 1 + 127, 0) - down, 1)
    scale = np.exp2(byte - 127.0)
    codes = (blocks / scale).astype(np.float32).astype(dtype).astype(np.float64)
    return np.moveaxis((codes * scale).reshape(v.shape), -1, axis)


WIDE = False


def mx_kscale(k):
    if not WIDE:
        return np.ones(k)
    levels = np.array([10, -10, 5, -5, 0])
    a = np.random.permutation(np.resize(levels, k // 512 * 4)).reshape(k // 512, 4)
    idx = np.arange(k)
    return np.exp2(a[idx // 512, idx % 128 // 32])


BF16 = ml_dtypes.bfloat16


def bf(x):
    return np.asarray(x, np.float32).astype(BF16)


def f64(x):
    return np.asarray(x).astype(np.float64)


T, B, F, H, R, O = 128, 8, 1024, 2048, 512, 128


def setup_inputs():
    s, t = mx_kscale(R), mx_kscale(H)
    return {"z2": bf(np.random.standard_normal((T, B, R)) * s),
            "sw1": bf(np.random.standard_normal((R, H)) / np.sqrt(R) / s[:, None] * t),
            "b2": bf(np.random.standard_normal((B, H)) * t),
            "w3": bf(np.random.standard_normal((B, H, O)) / np.sqrt(H) / t[:, None]),
            "b3": bf(np.random.standard_normal((B, O)))}


def reference(z2, sw1, b2, w3, b3):
    u = (mxq(f64(z2), 2, "e4m3").reshape(T * B, R) @ mxq(f64(sw1), 0, "e4m3")).reshape(T, B, H)
    h = np.maximum(u + f64(b2)[None, :, :], 0.0)
    out = (mxq(h, 2, "e4m3").transpose(1, 0, 2) @ mxq(f64(w3), 1, "e4m3")) + f64(b3)[:, None, :]
    return out.transpose(1, 0, 2)

@@ -1,0 +1,216 @@
+from contextlib import ExitStack
+
+import concourse.mybir as mybir
+from concourse.masks import make_identity
+
+BF16 = mybir.dt.bfloat16
+F32 = mybir.dt.float32
+U32 = mybir.dt.uint32
+U8 = mybir.dt.uint8
+FP8X4 = mybir.dt.float8_e4m3fn_x4
+RELU = mybir.ActivationFunctionType.Relu
+ADD = mybir.AluOpType.add
+
+T, B, R, H, O = 128, 8, 512, 2048, 128
+P = 128
+PACK = 4
+K_PASS = P * PACK
+G = H // K_PASS
+HALF = B // 2
+N_HALF = HALF * T
+SCALAR_SHARE = 32
+
+FLOPS = 2 * T * B * R * H + 2 * B * T * H * O
+
+
+def tile_mlpmodelpredictor_pb_kernel(tc, z2, sw1, b2, w3, b3, out):
+    nc = tc.nc
+    vector_share = P - SCALAR_SHARE
+    with ExitStack() as ctx:
+        keep = ctx.enter_context(tc.tile_pool(name="keep", bufs=1))
+        sw1_in = ctx.enter_context(tc.tile_pool(name="sw1_in", bufs=G))
+        w3_in = ctx.enter_context(tc.tile_pool(name="w3_in", bufs=B))
+        stage = ctx.enter_context(tc.tile_pool(name="stage", bufs=3))
+        banks = ctx.enter_context(tc.psum_pool(name="banks", bufs=6))
+        out_banks = ctx.enter_context(tc.psum_pool(name="out_banks", bufs=2))
+
+        b2_rows = keep.tile([P, K_PASS], BF16)
+        nc.scalar.dma_start(out=b2_rows[0 : B * G, :], in_=b2.rearrange("b (g x) -> (b g) x", g=G))
+        nc.vector.memset(b2_rows[32:64, :], 0.0)
+        nc.vector.memset(b2_rows[64:128, :], 0.0)
+
+        z2_raw = keep.tile([P, B, R], BF16)
+
+        sw1_pairs = sw1.rearrange("(u q e) h -> u q e h", u=2, e=2)
+        sw1_raw = []
+        for g in range(G):
+            raw = sw1_in.tile([P, PACK, K_PASS], BF16, name="sw1_raw")
+            for u in range(2):
+                nc.sync.dma_start(
+                    out=raw[:, 2 * u : 2 * u + 2, :],
+                    in_=sw1_pairs[u, :, :, g * K_PASS : (g + 1) * K_PASS],
+                )
+            sw1_raw.append(raw)
+            if g == 0:
+                nc.sync.dma_start(out=z2_raw[:, 0:HALF, :], in_=z2[:, 0:HALF, :])
+
+        nc.sync.dma_start(out=z2_raw[:, HALF:B, :], in_=z2[:, HALF:B, :])
+
+        w3_rows = w3.rearrange("b (g p j) o -> b p g (j o)", g=G, j=PACK)
+        w3_raw = []
+        for b in range(B):
+            raw = w3_in.tile([P, G, PACK, O], BF16, name="w3_raw")
+            nc.sync.dma_start(out=raw.rearrange("p g j o -> p g (j o)"), in_=w3_rows[b])
+            w3_raw.append(raw)
+
+        b3_all = keep.tile([P, B * O], BF16)
+        nc.sync.dma_start(out=b3_all[:], in_=b3.rearrange("b o -> (b o)").partition_broadcast(P))
+
+        ident = keep.tile([P, P], F32)
+        make_identity(nc, ident[:])
+        b2_sorted = keep.tile([P, PACK, P], F32)
+        nc.vector.tensor_copy(out=b2_sorted[:], in_=b2_rows.rearrange("r (q j) -> r j q", j=PACK))
+        b2_cols = keep.tile([P, PACK, B * G], F32)
+
+        def transpose_b2():
+            b2_bank = banks.tile([P, PACK, P], F32, tag="bank")
+            for j in range(PACK):
+                nc.tensor.transpose(b2_bank[:, j, :], b2_sorted[:, j, :], ident[:])
+            nc.scalar.copy(out=b2_cols[:], in_=b2_bank[:, :, 0 : B * G])
+
+        z_grouped = keep.tile([P, B, T, PACK], BF16, align_bytes=64)
+        z_codes = keep.tile([P, B * T], U32, align_bytes=64)
+        z_scales = keep.tile([P, B * T], U8, align_bytes=64)
+        sw1_codes = keep.tile([P, H], U32, align_bytes=64)
+        sw1_scales = keep.tile([P, H], U8, align_bytes=64)
+        w3_codes = keep.tile([P, B * G * O], U32, align_bytes=64)
+        w3_scales = keep.tile([P, B * G * O], U8, align_bytes=64)
+        h_codes = keep.tile([P, 2 * G * N_HALF], U32, align_bytes=64)
+        h_scales = keep.tile([P, 2 * G * N_HALF], U8, align_bytes=64)
+        out_sb = keep.tile([P, B * O], F32)
+
+        z2_words = z2_raw.bitcast(F32)
+        z_grouped_words = z_grouped.bitcast(F32)
+
+        def prepare_z2(half):
+            for pair in range(HALF // 2):
+                first = half * HALF + 2 * pair
+                zt = banks.tile([P, 2, 2, T], F32, tag="bank")
+                for d in range(2):
+                    for u in range(2):
+                        nc.tensor.transpose(
+                            zt[:, d, u, :], z2_words[:, first + d, u * P : (u + 1) * P], ident[:]
+                        )
+                nc.scalar.copy(
+                    out=z_grouped_words[:, first : first + 2, :, :],
+                    in_=zt.rearrange("p d u t -> p d t u"),
+                )
+            cols = slice(half * N_HALF, (half + 1) * N_HALF)
+            nc.vector.quantize_mx(
+                out=z_codes[:, cols].bitcast(FP8X4),
+                scales=z_scales[:, cols],
+                in_=z_grouped[:, half * HALF : (half + 1) * HALF].rearrange("p b t k -> p (b t k)"),
+            )
+
+        def prepare_sw1(g):
+            grouped = stage.tile([P, PACK, P, PACK], BF16, name="sw1_grouped", align_bytes=64)
+            source = sw1_raw[g].rearrange("p r (q j) -> p j q r", j=PACK)
+            nc.vector.tensor_copy(
+                out=grouped[:, :, 0:vector_share, :], in_=source[:, :, 0:vector_share, :]
+            )
+            nc.scalar.copy(out=grouped[:, :, vector_share:P, :], in_=source[:, :, vector_share:P, :])
+            cols = slice(g * K_PASS, (g + 1) * K_PASS)
+            nc.vector.quantize_mx(
+                out=sw1_codes[:, cols].bitcast(FP8X4),
+                scales=sw1_scales[:, cols],
+                in_=grouped.rearrange("p j q r -> p (j q r)"),
+            )
+
+        def prepare_w3(b):
+            grouped = stage.tile([P, G, O, PACK], BF16, name="w3_grouped", align_bytes=64)
+            nc.vector.tensor_copy(
+                out=grouped[:, :, 0:vector_share, :].rearrange("p g (c i) j -> p g c j i", i=4),
+                in_=w3_raw[b][:, :, :, 0:vector_share].rearrange("p g j (c i) -> p g c j i", i=4),
+            )
+            nc.scalar.copy(
+                out=grouped[:, :, vector_share:O, :],
+                in_=w3_raw[b][:, :, :, vector_share:O].rearrange("p g j o -> p g o j"),
+            )
+            cols = slice(b * G * O, (b + 1) * G * O)
+            nc.vector.quantize_mx(
+                out=w3_codes[:, cols].bitcast(FP8X4),
+                scales=w3_scales[:, cols],
+                in_=grouped.rearrange("p g o j -> p (g o j)"),
+            )
+
+        def hidden_layer(half, g):
+            z_cols = slice(half * N_HALF, (half + 1) * N_HALF)
+            planes = stage.tile([P, PACK, N_HALF], BF16, name="h_planes")
+            for j in range(PACK):
+                w_cols = slice((g * PACK + j) * P, (g * PACK + j + 1) * P)
+                u_bank = banks.tile([P, N_HALF], F32, tag="bank")
+                nc.tensor.matmul_mx(
+                    out=u_bank[:],
+                    lhsT=sw1_codes[:, w_cols].bitcast(FP8X4),
+                    lhsT_scale=sw1_scales[:, w_cols],
+                    rhs=z_codes[:, z_cols].bitcast(FP8X4),
+                    rhs_scale=z_scales[:, z_cols],
+                    start=True,
+                    stop=True,
+                )
+                for d in range(HALF):
+                    bias_col = (half * HALF + d) * G + g
+                    nc.scalar.activation(
+                        out=planes[:, j, d * T : (d + 1) * T],
+                        in_=u_bank[:, d * T : (d + 1) * T],
+                        func=RELU,
+                        bias=b2_cols[:, j, bias_col : bias_col + 1],
+                        scale=1.0,
+                    )
+            grouped = stage.tile([P, N_HALF, PACK], BF16, name="h_grouped", align_bytes=64)
+            nc.vector.tensor_copy(
+                out=grouped.rearrange("p (c i) j -> p c j i", i=4),
+                in_=planes.rearrange("p j (c i) -> p c j i", i=4),
+            )
+            for d in range(HALF):
+                first = (half * G + g) * N_HALF + d * T
+                nc.vector.quantize_mx(
+                    out=h_codes[:, first : first + T].bitcast(FP8X4),
+                    scales=h_scales[:, first : first + T],
+                    in_=grouped[:, d * T : (d + 1) * T, :].rearrange("p n j -> p (n j)"),
+                )
+
+        def output_layer(half):
+            o_bank = out_banks.tile([P, HALF * O], F32)
+            for d in range(HALF):
+                b = half * HALF + d
+                for g in range(G):
+                    h_cols = slice((half * G + g) * N_HALF + d * T, (half * G + g) * N_HALF + (d + 1) * T)
+                    w_cols = slice((b * G + g) * O, (b * G + g + 1) * O)
+                    nc.tensor.matmul_mx(
+                        out=o_bank[:, d * O : (d + 1) * O],
+                        lhsT=h_codes[:, h_cols].bitcast(FP8X4),
+                        lhsT_scale=h_scales[:, h_cols],
+                        rhs=w3_codes[:, w_cols].bitcast(FP8X4),
+                        rhs_scale=w3_scales[:, w_cols],
+                        start=(g == 0),
+                        stop=(g == G - 1),
+                    )
+            cols = slice(half * HALF * O, (half + 1) * HALF * O)
+            nc.vector.tensor_tensor(out=out_sb[:, cols], in0=o_bank[:], in1=b3_all[:, cols], op=ADD)
+            nc.sync.dma_start(
+                out=out[:, half * HALF : (half + 1) * HALF, :].rearrange("t b o -> t (b o)"),
+                in_=out_sb[:, cols],
+            )
+
+        prepare_z2(0)
+        transpose_b2()
+        for half in range(2):
+            for g in range(G):
+                if half == 0:
+                    prepare_sw1(g)
+                hidden_layer(half, g)
+                prepare_w3(half * G + g)
+                if half == 0 and g == 1:
+                    prepare_z2(1)
+            output_layer(half)

@@ -18,7 +18,7 @@ K_PASS = P * PACK
 G = H // K_PASS
 HALF = B // 2
 N_HALF = HALF * T
-SCALAR_SHARE = 32
+SCALAR_SHARE = 8
 
 FLOPS = 2 * T * B * R * H + 2 * B * T * H * O
 

@@ -18,21 +18,24 @@ K_PASS = P * PACK
 G = H // K_PASS
 HALF = B // 2
 N_HALF = HALF * T
-SCALAR_SHARE = 8
+UNITS = 2 * G
+SCALAR_SHARE = 32
 
 FLOPS = 2 * T * B * R * H + 2 * B * T * H * O
 
 
 def tile_mlpmodelpredictor_pb_kernel(tc, z2, sw1, b2, w3, b3, out):
     nc = tc.nc
-    vector_share = P - SCALAR_SHARE
+    vector_share = O - SCALAR_SHARE
     with ExitStack() as ctx:
         keep = ctx.enter_context(tc.tile_pool(name="keep", bufs=1))
         sw1_in = ctx.enter_context(tc.tile_pool(name="sw1_in", bufs=G))
         w3_in = ctx.enter_context(tc.tile_pool(name="w3_in", bufs=B))
-        stage = ctx.enter_context(tc.tile_pool(name="stage", bufs=3))
+        stage = ctx.enter_context(tc.tile_pool(name="stage", bufs=2))
+        plane_pool = ctx.enter_context(tc.tile_pool(name="plane_pool", bufs=4))
         banks = ctx.enter_context(tc.psum_pool(name="banks", bufs=6))
         out_banks = ctx.enter_context(tc.psum_pool(name="out_banks", bufs=2))
+        ctx.enter_context(tc.manual_schedule())
 
         b2_rows = keep.tile([P, K_PASS], BF16)
         nc.scalar.dma_start(out=b2_rows[0 : B * G, :], in_=b2.rearrange("b (g x) -> (b g) x", g=G))
@@ -85,14 +88,22 @@ def tile_mlpmodelpredictor_pb_kernel(tc, z2, sw1, b2, w3, b3, out):
         sw1_scales = keep.tile([P, H], U8, align_bytes=64)
         w3_codes = keep.tile([P, B * G * O], U32, align_bytes=64)
         w3_scales = keep.tile([P, B * G * O], U8, align_bytes=64)
-        h_codes = keep.tile([P, 2 * G * N_HALF], U32, align_bytes=64)
-        h_scales = keep.tile([P, 2 * G * N_HALF], U8, align_bytes=64)
+        h_codes = keep.tile([P, UNITS * N_HALF], U32, align_bytes=64)
+        h_scales = keep.tile([P, UNITS * N_HALF], U8, align_bytes=64)
         out_sb = keep.tile([P, B * O], F32)
 
         z2_words = z2_raw.bitcast(F32)
         z_grouped_words = z_grouped.bitcast(F32)
 
-        def prepare_z2(half):
+        def quantise(codes, scales, first, grouped):
+            n = grouped.shape[1] // PACK
+            nc.vector.quantize_mx(
+                out=codes[:, first : first + n].bitcast(FP8X4),
+                scales=scales[:, first : first + n],
+                in_=grouped,
+            )
+
+        def transpose_z2(half):
             for pair in range(HALF // 2):
                 first = half * HALF + 2 * pair
                 zt = banks.tile([P, 2, 2, T], F32, tag="bank")
@@ -105,28 +116,23 @@ def tile_mlpmodelpredictor_pb_kernel(tc, z2, sw1, b2, w3, b3, out):
                     out=z_grouped_words[:, first : first + 2, :, :],
                     in_=zt.rearrange("p d u t -> p d t u"),
                 )
-            cols = slice(half * N_HALF, (half + 1) * N_HALF)
-            nc.vector.quantize_mx(
-                out=z_codes[:, cols].bitcast(FP8X4),
-                scales=z_scales[:, cols],
-                in_=z_grouped[:, half * HALF : (half + 1) * HALF].rearrange("p b t k -> p (b t k)"),
+
+        def quantise_z2(half):
+            quantise(
+                z_codes,
+                z_scales,
+                half * N_HALF,
+                z_grouped[:, half * HALF : (half + 1) * HALF].rearrange("p b t k -> p (b t k)"),
             )
 
-        def prepare_sw1(g):
+        def regroup_sw1(g):
             grouped = stage.tile([P, PACK, P, PACK], BF16, name="sw1_grouped", align_bytes=64)
-            source = sw1_raw[g].rearrange("p r (q j) -> p j q r", j=PACK)
             nc.vector.tensor_copy(
-                out=grouped[:, :, 0:vector_share, :], in_=source[:, :, 0:vector_share, :]
+                out=grouped[:], in_=sw1_raw[g].rearrange("p r (q j) -> p j q r", j=PACK)
             )
-            nc.scalar.copy(out=grouped[:, :, vector_share:P, :], in_=source[:, :, vector_share:P, :])
-            cols = slice(g * K_PASS, (g + 1) * K_PASS)
-            nc.vector.quantize_mx(
-                out=sw1_codes[:, cols].bitcast(FP8X4),
-                scales=sw1_scales[:, cols],
-                in_=grouped.rearrange("p j q r -> p (j q r)"),
-            )
+            return grouped.rearrange("p j q r -> p (j q r)")
 
-        def prepare_w3(b):
+        def regroup_w3(b):
             grouped = stage.tile([P, G, O, PACK], BF16, name="w3_grouped", align_bytes=64)
             nc.vector.tensor_copy(
                 out=grouped[:, :, 0:vector_share, :].rearrange("p g (c i) j -> p g c j i", i=4),
@@ -136,16 +142,12 @@ def tile_mlpmodelpredictor_pb_kernel(tc, z2, sw1, b2, w3, b3, out):
                 out=grouped[:, :, vector_share:O, :],
                 in_=w3_raw[b][:, :, :, vector_share:O].rearrange("p g j o -> p g o j"),
             )
-            cols = slice(b * G * O, (b + 1) * G * O)
-            nc.vector.quantize_mx(
-                out=w3_codes[:, cols].bitcast(FP8X4),
-                scales=w3_scales[:, cols],
-                in_=grouped.rearrange("p g o j -> p (g o j)"),
-            )
+            return grouped.rearrange("p g o j -> p (g o j)")
 
-        def hidden_layer(half, g):
+        def hidden_matmuls(unit):
+            half, g = divmod(unit, G)
             z_cols = slice(half * N_HALF, (half + 1) * N_HALF)
-            planes = stage.tile([P, PACK, N_HALF], BF16, name="h_planes")
+            planes = plane_pool.tile([P, PACK, N_HALF], BF16, name="h_planes")
             for j in range(PACK):
                 w_cols = slice((g * PACK + j) * P, (g * PACK + j + 1) * P)
                 u_bank = banks.tile([P, N_HALF], F32, tag="bank")
@@ -167,17 +169,23 @@ def tile_mlpmodelpredictor_pb_kernel(tc, z2, sw1, b2, w3, b3, out):
                         bias=b2_cols[:, j, bias_col : bias_col + 1],
                         scale=1.0,
                     )
+            return planes
+
+        def regroup_h(planes):
             grouped = stage.tile([P, N_HALF, PACK], BF16, name="h_grouped", align_bytes=64)
             nc.vector.tensor_copy(
                 out=grouped.rearrange("p (c i) j -> p c j i", i=4),
                 in_=planes.rearrange("p j (c i) -> p c j i", i=4),
             )
+            return grouped
+
+        def quantise_h(unit, grouped):
             for d in range(HALF):
-                first = (half * G + g) * N_HALF + d * T
-                nc.vector.quantize_mx(
-                    out=h_codes[:, first : first + T].bitcast(FP8X4),
-                    scales=h_scales[:, first : first + T],
-                    in_=grouped[:, d * T : (d + 1) * T, :].rearrange("p n j -> p (n j)"),
+                quantise(
+                    h_codes,
+                    h_scales,
+                    unit * N_HALF + d * T,
+                    grouped[:, d * T : (d + 1) * T, :].rearrange("p n j -> p (n j)"),
                 )
 
         def output_layer(half):
@@ -185,14 +193,14 @@ def tile_mlpmodelpredictor_pb_kernel(tc, z2, sw1, b2, w3, b3, out):
             for d in range(HALF):
                 b = half * HALF + d
                 for g in range(G):
-                    h_cols = slice((half * G + g) * N_HALF + d * T, (half * G + g) * N_HALF + (d + 1) * T)
-                    w_cols = slice((b * G + g) * O, (b * G + g + 1) * O)
+                    h_first = (half * G + g) * N_HALF + d * T
+                    w_first = (b * G + g) * O
                     nc.tensor.matmul_mx(
                         out=o_bank[:, d * O : (d + 1) * O],
-                        lhsT=h_codes[:, h_cols].bitcast(FP8X4),
-                        lhsT_scale=h_scales[:, h_cols],
-                        rhs=w3_codes[:, w_cols].bitcast(FP8X4),
-                        rhs_scale=w3_scales[:, w_cols],
+                        lhsT=h_codes[:, h_first : h_first + T].bitcast(FP8X4),
+                        lhsT_scale=h_scales[:, h_first : h_first + T],
+                        rhs=w3_codes[:, w_first : w_first + O].bitcast(FP8X4),
+                        rhs_scale=w3_scales[:, w_first : w_first + O],
                         start=(g == 0),
                         stop=(g == G - 1),
                     )
@@ -203,14 +211,27 @@ def tile_mlpmodelpredictor_pb_kernel(tc, z2, sw1, b2, w3, b3, out):
                 in_=out_sb[:, cols],
             )
 
-        prepare_z2(0)
+        transpose_z2(0)
         transpose_b2()
-        for half in range(2):
-            for g in range(G):
-                if half == 0:
-                    prepare_sw1(g)
-                hidden_layer(half, g)
-                prepare_w3(half * G + g)
-                if half == 0 and g == 1:
-                    prepare_z2(1)
-            output_layer(half)
+        grouped_now = regroup_sw1(0)
+        quantise(sw1_codes, sw1_scales, 0, grouped_now)
+        grouped_now = regroup_sw1(1)
+        quantise_z2(0)
+        for g in range(1, G):
+            grouped_next = regroup_sw1(g + 1) if g + 1 < G else None
+            quantise(sw1_codes, sw1_scales, g * K_PASS, grouped_now)
+            grouped_now = grouped_next
+
+        for unit in range(UNITS):
+            planes = hidden_matmuls(unit)
+            if unit == 0:
+                transpose_z2(1)
+            w3_grouped = regroup_w3(unit)
+            if unit == UNITS - 1:
+                output_layer(0)
+            h_grouped = regroup_h(planes)
+            if unit == 1:
+                quantise_z2(1)
+            quantise(w3_codes, w3_scales, unit * G * O, w3_grouped)
+            quantise_h(unit, h_grouped)
+        output_layer(1)

@@ -19,7 +19,7 @@ G = H // K_PASS
 HALF = B // 2
 N_HALF = HALF * T
 UNITS = 2 * G
-SCALAR_SHARE = 32
+SCALAR_SHARE = 64
 
 FLOPS = 2 * T * B * R * H + 2 * B * T * H * O
 

@@ -19,7 +19,8 @@ G = H // K_PASS
 HALF = B // 2
 N_HALF = HALF * T
 UNITS = 2 * G
-SCALAR_SHARE = 64
+SCALAR_SHARE = 44
+EARLY_CHUNKS = 2
 
 FLOPS = 2 * T * B * R * H + 2 * B * T * H * O
 
@@ -127,9 +128,11 @@ def tile_mlpmodelpredictor_pb_kernel(tc, z2, sw1, b2, w3, b3, out):
 
         def regroup_sw1(g):
             grouped = stage.tile([P, PACK, P, PACK], BF16, name="sw1_grouped", align_bytes=64)
-            nc.vector.tensor_copy(
-                out=grouped[:], in_=sw1_raw[g].rearrange("p r (q j) -> p j q r", j=PACK)
-            )
+            source = sw1_raw[g].rearrange("p r (q j) -> p j q r", j=PACK)
+            vector_q = P // 2 if g < EARLY_CHUNKS else P
+            nc.vector.tensor_copy(out=grouped[:, :, 0:vector_q, :], in_=source[:, :, 0:vector_q, :])
+            if vector_q < P:
+                nc.scalar.copy(out=grouped[:, :, vector_q:P, :], in_=source[:, :, vector_q:P, :])
             return grouped.rearrange("p j q r -> p (j q r)")
 
         def regroup_w3(b):
@@ -211,9 +214,9 @@ def tile_mlpmodelpredictor_pb_kernel(tc, z2, sw1, b2, w3, b3, out):
                 in_=out_sb[:, cols],
             )
 
+        grouped_now = regroup_sw1(0)
         transpose_z2(0)
         transpose_b2()
-        grouped_now = regroup_sw1(0)
         quantise(sw1_codes, sw1_scales, 0, grouped_now)
         grouped_now = regroup_sw1(1)
         quantise_z2(0)

@@ -43,6 +43,10 @@ def tile_mlpmodelpredictor_pb_kernel(tc, z2, sw1, b2, w3, b3, out):
         nc.vector.memset(b2_rows[32:64, :], 0.0)
         nc.vector.memset(b2_rows[64:128, :], 0.0)
 
+        warm = keep.tile([P, 2], F32)
+        nc.vector.memset(warm[:], 0.0)
+        nc.scalar.activation(out=warm[:, 1:2], in_=warm[:, 0:1], func=RELU)
+
         z2_raw = keep.tile([P, B, R], BF16)
 
         sw1_pairs = sw1.rearrange("(u q e) h -> u q e h", u=2, e=2)

@@ -19,7 +19,7 @@ G = H // K_PASS
 HALF = B // 2
 N_HALF = HALF * T
 UNITS = 2 * G
-SCALAR_SHARE = 44
+TE_G = 2
 EARLY_CHUNKS = 2
 
 FLOPS = 2 * T * B * R * H + 2 * B * T * H * O
@@ -27,14 +27,14 @@ FLOPS = 2 * T * B * R * H + 2 * B * T * H * O
 
 def tile_mlpmodelpredictor_pb_kernel(tc, z2, sw1, b2, w3, b3, out):
     nc = tc.nc
-    vector_share = O - SCALAR_SHARE
     with ExitStack() as ctx:
         keep = ctx.enter_context(tc.tile_pool(name="keep", bufs=1))
         sw1_in = ctx.enter_context(tc.tile_pool(name="sw1_in", bufs=G))
         w3_in = ctx.enter_context(tc.tile_pool(name="w3_in", bufs=B))
         stage = ctx.enter_context(tc.tile_pool(name="stage", bufs=2))
         plane_pool = ctx.enter_context(tc.tile_pool(name="plane_pool", bufs=4))
-        banks = ctx.enter_context(tc.psum_pool(name="banks", bufs=6))
+        banks = ctx.enter_context(tc.psum_pool(name="banks", bufs=4))
+        w3_banks = ctx.enter_context(tc.psum_pool(name="w3_banks", bufs=2))
         out_banks = ctx.enter_context(tc.psum_pool(name="out_banks", bufs=2))
         ctx.enter_context(tc.manual_schedule())
 
@@ -76,6 +76,8 @@ def tile_mlpmodelpredictor_pb_kernel(tc, z2, sw1, b2, w3, b3, out):
 
         ident = keep.tile([P, P], F32)
         make_identity(nc, ident[:])
+        ident_bf = keep.tile([P, P], BF16)
+        make_identity(nc, ident_bf[:])
         b2_sorted = keep.tile([P, PACK, P], F32)
         nc.vector.tensor_copy(out=b2_sorted[:], in_=b2_rows.rearrange("r (q j) -> r j q", j=PACK))
         b2_cols = keep.tile([P, PACK, B * G], F32)
@@ -141,13 +143,19 @@ def tile_mlpmodelpredictor_pb_kernel(tc, z2, sw1, b2, w3, b3, out):
 
         def regroup_w3(b):
             grouped = stage.tile([P, G, O, PACK], BF16, name="w3_grouped", align_bytes=64)
+            bank = w3_banks.tile([P, TE_G, O, PACK], BF16)
+            for g in range(TE_G):
+                nc.tensor.matmul(
+                    bank[:, g],
+                    lhsT=ident_bf[:],
+                    rhs=w3_raw[b][:, g].rearrange("p j o -> p o j"),
+                    start=True,
+                    stop=True,
+                )
+            nc.scalar.copy(out=grouped[:, 0:TE_G], in_=bank[:])
             nc.vector.tensor_copy(
-                out=grouped[:, :, 0:vector_share, :].rearrange("p g (c i) j -> p g c j i", i=4),
-                in_=w3_raw[b][:, :, :, 0:vector_share].rearrange("p g j (c i) -> p g c j i", i=4),
-            )
-            nc.scalar.copy(
-                out=grouped[:, :, vector_share:O, :],
-                in_=w3_raw[b][:, :, :, vector_share:O].rearrange("p g j o -> p g o j"),
+                out=grouped[:, TE_G:G].rearrange("p g (c i) j -> p g c j i", i=4),
+                in_=w3_raw[b][:, TE_G:G].rearrange("p g j (c i) -> p g c j i", i=4),
             )
             return grouped.rearrange("p g o j -> p (g o j)")
 

@@ -18,9 +18,10 @@ K_PASS = P * PACK
 G = H // K_PASS
 HALF = B // 2
 N_HALF = HALF * T
-UNITS = 2 * G
+V_SLOTS = 3
 TE_G = 2
-EARLY_CHUNKS = 2
+
+S_COLS = 0
 
 FLOPS = 2 * T * B * R * H + 2 * B * T * H * O
 
@@ -31,8 +32,10 @@ def tile_mlpmodelpredictor_pb_kernel(tc, z2, sw1, b2, w3, b3, out):
         keep = ctx.enter_context(tc.tile_pool(name="keep", bufs=1))
         sw1_in = ctx.enter_context(tc.tile_pool(name="sw1_in", bufs=G))
         w3_in = ctx.enter_context(tc.tile_pool(name="w3_in", bufs=B))
-        stage = ctx.enter_context(tc.tile_pool(name="stage", bufs=2))
-        plane_pool = ctx.enter_context(tc.tile_pool(name="plane_pool", bufs=4))
+        sw1_stage = ctx.enter_context(tc.tile_pool(name="sw1_stage", bufs=G))
+        w3_stage = ctx.enter_context(tc.tile_pool(name="w3_stage", bufs=4))
+        stage = ctx.enter_context(tc.tile_pool(name="stage", bufs=3))
+        plane_pool = ctx.enter_context(tc.tile_pool(name="plane_pool", bufs=6))
         banks = ctx.enter_context(tc.psum_pool(name="banks", bufs=4))
         w3_banks = ctx.enter_context(tc.psum_pool(name="w3_banks", bufs=2))
         out_banks = ctx.enter_context(tc.psum_pool(name="out_banks", bufs=2))
@@ -49,6 +52,11 @@ def tile_mlpmodelpredictor_pb_kernel(tc, z2, sw1, b2, w3, b3, out):
 
         z2_raw = keep.tile([P, B, R], BF16)
 
+        def load_z2(pair):
+            nc.sync.dma_start(
+                out=z2_raw[:, 2 * pair : 2 * pair + 2, :], in_=z2[:, 2 * pair : 2 * pair + 2, :]
+            )
+
         sw1_pairs = sw1.rearrange("(u q e) h -> u q e h", u=2, e=2)
         sw1_raw = []
         for g in range(G):
@@ -60,9 +68,10 @@ def tile_mlpmodelpredictor_pb_kernel(tc, z2, sw1, b2, w3, b3, out):
                 )
             sw1_raw.append(raw)
             if g == 0:
-                nc.sync.dma_start(out=z2_raw[:, 0:HALF, :], in_=z2[:, 0:HALF, :])
-
-        nc.sync.dma_start(out=z2_raw[:, HALF:B, :], in_=z2[:, HALF:B, :])
+                load_z2(0)
+                load_z2(1)
+        load_z2(2)
+        load_z2(3)
 
         w3_rows = w3.rearrange("b (g p j) o -> b p g (j o)", g=G, j=PACK)
         w3_raw = []
@@ -95,8 +104,8 @@ def tile_mlpmodelpredictor_pb_kernel(tc, z2, sw1, b2, w3, b3, out):
         sw1_scales = keep.tile([P, H], U8, align_bytes=64)
         w3_codes = keep.tile([P, B * G * O], U32, align_bytes=64)
         w3_scales = keep.tile([P, B * G * O], U8, align_bytes=64)
-        h_codes = keep.tile([P, UNITS * N_HALF], U32, align_bytes=64)
-        h_scales = keep.tile([P, UNITS * N_HALF], U8, align_bytes=64)
+        h_codes = keep.tile([P, B * G * T], U32, align_bytes=64)
+        h_scales = keep.tile([P, B * G * T], U8, align_bytes=64)
         out_sb = keep.tile([P, B * O], F32)
 
         z2_words = z2_raw.bitcast(F32)
@@ -110,39 +119,55 @@ def tile_mlpmodelpredictor_pb_kernel(tc, z2, sw1, b2, w3, b3, out):
                 in_=grouped,
             )
 
-        def transpose_z2(half):
-            for pair in range(HALF // 2):
-                first = half * HALF + 2 * pair
-                zt = banks.tile([P, 2, 2, T], F32, tag="bank")
-                for d in range(2):
-                    for u in range(2):
-                        nc.tensor.transpose(
-                            zt[:, d, u, :], z2_words[:, first + d, u * P : (u + 1) * P], ident[:]
-                        )
-                nc.scalar.copy(
-                    out=z_grouped_words[:, first : first + 2, :, :],
-                    in_=zt.rearrange("p d u t -> p d t u"),
-                )
-
-        def quantise_z2(half):
-            quantise(
-                z_codes,
-                z_scales,
-                half * N_HALF,
-                z_grouped[:, half * HALF : (half + 1) * HALF].rearrange("p b t k -> p (b t k)"),
+        def transpose_z2(pair):
+            zt = banks.tile([P, 2, 2, T], F32, tag="bank")
+            for d in range(2):
+                for u in range(2):
+                    nc.tensor.transpose(
+                        zt[:, d, u, :], z2_words[:, 2 * pair + d, u * P : (u + 1) * P], ident[:]
+                    )
+            nc.scalar.copy(
+                out=z_grouped_words[:, 2 * pair : 2 * pair + 2, :, :],
+                in_=zt.rearrange("p d u t -> p d t u"),
             )
 
-        def regroup_sw1(g):
-            grouped = stage.tile([P, PACK, P, PACK], BF16, name="sw1_grouped", align_bytes=64)
-            source = sw1_raw[g].rearrange("p r (q j) -> p j q r", j=PACK)
-            vector_q = P // 2 if g < EARLY_CHUNKS else P
-            nc.vector.tensor_copy(out=grouped[:, :, 0:vector_q, :], in_=source[:, :, 0:vector_q, :])
-            if vector_q < P:
-                nc.scalar.copy(out=grouped[:, :, vector_q:P, :], in_=source[:, :, vector_q:P, :])
-            return grouped.rearrange("p j q r -> p (j q r)")
+        def quantise_z2(b0, b1):
+            quantise(
+                z_codes, z_scales, b0 * T, z_grouped[:, b0:b1].rearrange("p b t k -> p (b t k)")
+            )
 
-        def regroup_w3(b):
-            grouped = stage.tile([P, G, O, PACK], BF16, name="w3_grouped", align_bytes=64)
+        sw1_grouped = {}
+
+        for g in range(G):
+            sw1_grouped[g] = sw1_stage.tile([P, PACK, P, PACK], BF16, name="sw1_stage", align_bytes=64)
+
+        def sw1_slots(g, j0, j1):
+            source = sw1_raw[g].rearrange("p r (q j) -> p j q r", j=PACK)
+            return {"out": sw1_grouped[g][:, j0:j1], "in_": source[:, j0:j1]}
+
+        def regroup_sw1(g, j0=0, j1=V_SLOTS):
+            nc.vector.tensor_copy(**sw1_slots(g, j0, j1))
+
+        def scalar_regroup_sw1(g):
+            nc.scalar.copy(**sw1_slots(g, V_SLOTS, PACK))
+
+        def quantise_sw1(g, j0=0, j1=PACK):
+            quantise(
+                sw1_codes,
+                sw1_scales,
+                g * K_PASS + j0 * P,
+                sw1_grouped[g][:, j0:j1].rearrange("p j q r -> p (j q r)"),
+            )
+
+        w3_grouped = {}
+
+        def w3_stage_of(b):
+            if b not in w3_grouped:
+                w3_grouped[b] = w3_stage.tile([P, G, O, PACK], BF16, name="w3_stage", align_bytes=64)
+            return w3_grouped[b]
+
+        def spread_w3(b):
+            grouped = w3_stage_of(b)
             bank = w3_banks.tile([P, TE_G, O, PACK], BF16)
             for g in range(TE_G):
                 nc.tensor.matmul(
@@ -153,100 +178,211 @@ def tile_mlpmodelpredictor_pb_kernel(tc, z2, sw1, b2, w3, b3, out):
                     stop=True,
                 )
             nc.scalar.copy(out=grouped[:, 0:TE_G], in_=bank[:])
-            nc.vector.tensor_copy(
-                out=grouped[:, TE_G:G].rearrange("p g (c i) j -> p g c j i", i=4),
-                in_=w3_raw[b][:, TE_G:G].rearrange("p g j (c i) -> p g c j i", i=4),
-            )
-            return grouped.rearrange("p g o j -> p (g o j)")
+            if S_COLS:
+                nc.scalar.copy(
+                    out=grouped[:, TE_G:G, 0:S_COLS],
+                    in_=w3_raw[b][:, TE_G:G, :, 0:S_COLS].rearrange("p g j o -> p g o j"),
+                )
 
-        def hidden_matmuls(unit):
-            half, g = divmod(unit, G)
-            z_cols = slice(half * N_HALF, (half + 1) * N_HALF)
-            planes = plane_pool.tile([P, PACK, N_HALF], BF16, name="h_planes")
-            for j in range(PACK):
+        def regroup_w3(b):
+            nc.vector.tensor_copy(
+                out=w3_stage_of(b)[:, TE_G:G, S_COLS:O].rearrange("p g (c i) j -> p g c j i", i=4),
+                in_=w3_raw[b][:, TE_G:G, :, S_COLS:O].rearrange("p g j (c i) -> p g c j i", i=4),
+            )
+
+        def quantise_w3(b):
+            quantise(
+                w3_codes, w3_scales, b * G * O, w3_grouped[b].rearrange("p g o j -> p (g o j)")
+            )
+
+        planes_of = {}
+        grouped_of = {}
+
+        def relu_out(plane, bank, j, b, g):
+            nc.scalar.activation(
+                out=plane, in_=bank, func=RELU, bias=b2_cols[:, j, b * G + g : b * G + g + 1], scale=1.0
+            )
+
+        def hidden_half(g, slots=range(PACK), b0=0, b1=HALF):
+            if ("half", g) not in planes_of:
+                planes_of["half", g] = plane_pool.tile([P, PACK, N_HALF], BF16, name="h_planes")
+            planes = planes_of["half", g]
+            for j in slots:
                 w_cols = slice((g * PACK + j) * P, (g * PACK + j + 1) * P)
-                u_bank = banks.tile([P, N_HALF], F32, tag="bank")
+                bank = banks.tile([P, HALF, T], F32, tag="bank")
                 nc.tensor.matmul_mx(
-                    out=u_bank[:],
+                    out=bank[:, 0 : b1 - b0].rearrange("p b t -> p (b t)"),
                     lhsT=sw1_codes[:, w_cols].bitcast(FP8X4),
                     lhsT_scale=sw1_scales[:, w_cols],
-                    rhs=z_codes[:, z_cols].bitcast(FP8X4),
-                    rhs_scale=z_scales[:, z_cols],
+                    rhs=z_codes[:, b0 * T : b1 * T].bitcast(FP8X4),
+                    rhs_scale=z_scales[:, b0 * T : b1 * T],
                     start=True,
                     stop=True,
                 )
-                for d in range(HALF):
-                    bias_col = (half * HALF + d) * G + g
-                    nc.scalar.activation(
-                        out=planes[:, j, d * T : (d + 1) * T],
-                        in_=u_bank[:, d * T : (d + 1) * T],
-                        func=RELU,
-                        bias=b2_cols[:, j, bias_col : bias_col + 1],
-                        scale=1.0,
-                    )
-            return planes
+                for b in range(b0, b1):
+                    relu_out(planes[:, j, b * T : (b + 1) * T], bank[:, b - b0], j, b, g)
 
-        def regroup_h(planes):
-            grouped = stage.tile([P, N_HALF, PACK], BF16, name="h_grouped", align_bytes=64)
+        def regroup_half(g):
+            grouped = stage.tile([P, N_HALF, PACK], BF16, name="h_stage", align_bytes=64)
             nc.vector.tensor_copy(
                 out=grouped.rearrange("p (c i) j -> p c j i", i=4),
-                in_=planes.rearrange("p j (c i) -> p c j i", i=4),
+                in_=planes_of["half", g].rearrange("p j (c i) -> p c j i", i=4),
             )
-            return grouped
+            grouped_of["half", g] = grouped
 
-        def quantise_h(unit, grouped):
-            for d in range(HALF):
-                quantise(
-                    h_codes,
-                    h_scales,
-                    unit * N_HALF + d * T,
-                    grouped[:, d * T : (d + 1) * T, :].rearrange("p n j -> p (n j)"),
+        def quantise_half(g):
+            quantise(h_codes, h_scales, g * N_HALF, grouped_of["half", g].rearrange("p n j -> p (n j)"))
+
+        def hidden_one(b, g0, g1):
+            z_cols = slice(b * T, (b + 1) * T)
+            planes = plane_pool.tile([P, g1 - g0, PACK, T], BF16, name="h_planes")
+            for g in range(g0, g1):
+                bank = banks.tile([P, PACK, T], F32, tag="bank")
+                for j in range(PACK):
+                    w_cols = slice((g * PACK + j) * P, (g * PACK + j + 1) * P)
+                    nc.tensor.matmul_mx(
+                        out=bank[:, j],
+                        lhsT=sw1_codes[:, w_cols].bitcast(FP8X4),
+                        lhsT_scale=sw1_scales[:, w_cols],
+                        rhs=z_codes[:, z_cols].bitcast(FP8X4),
+                        rhs_scale=z_scales[:, z_cols],
+                        start=True,
+                        stop=True,
+                    )
+                for j in range(PACK):
+                    relu_out(planes[:, g - g0, j], bank[:, j], j, b, g)
+            planes_of[b, g0] = planes
+
+        def regroup_one(b, g0, g1):
+            grouped = stage.tile([P, g1 - g0, T, PACK], BF16, name="h_stage", align_bytes=64)
+            nc.vector.tensor_copy(
+                out=grouped.rearrange("p g (c i) j -> p g c j i", i=4),
+                in_=planes_of[b, g0].rearrange("p g j (c i) -> p g c j i", i=4),
+            )
+            grouped_of[b, g0] = grouped
+
+        def quantise_one(b, g0, g1):
+            quantise(
+                h_codes,
+                h_scales,
+                (b * G + g0) * T,
+                grouped_of[b, g0].rearrange("p g n j -> p (g n j)"),
+            )
+
+        def output_passes(o_out, b, gs):
+            for g in gs:
+                h_first = g * N_HALF + b * T if b < HALF else (b * G + g) * T
+                w_first = (b * G + g) * O
+                nc.tensor.matmul_mx(
+                    out=o_out,
+                    lhsT=h_codes[:, h_first : h_first + T].bitcast(FP8X4),
+                    lhsT_scale=h_scales[:, h_first : h_first + T],
+                    rhs=w3_codes[:, w_first : w_first + O].bitcast(FP8X4),
+                    rhs_scale=w3_scales[:, w_first : w_first + O],
+                    start=(g == 0),
+                    stop=(g == G - 1),
                 )
 
-        def output_layer(half):
-            o_bank = out_banks.tile([P, HALF * O], F32)
-            for d in range(HALF):
-                b = half * HALF + d
-                for g in range(G):
-                    h_first = (half * G + g) * N_HALF + d * T
-                    w_first = (b * G + g) * O
-                    nc.tensor.matmul_mx(
-                        out=o_bank[:, d * O : (d + 1) * O],
-                        lhsT=h_codes[:, h_first : h_first + T].bitcast(FP8X4),
-                        lhsT_scale=h_scales[:, h_first : h_first + T],
-                        rhs=w3_codes[:, w_first : w_first + O].bitcast(FP8X4),
-                        rhs_scale=w3_scales[:, w_first : w_first + O],
-                        start=(g == 0),
-                        stop=(g == G - 1),
-                    )
-            cols = slice(half * HALF * O, (half + 1) * HALF * O)
-            nc.vector.tensor_tensor(out=out_sb[:, cols], in0=o_bank[:], in1=b3_all[:, cols], op=ADD)
+        o_bank_of = {}
+
+        def multiply_out(b0, b1):
+            o_bank = out_banks.tile([P, HALF, O], F32, name="o_bank")
+            for b in range(b0, b1):
+                output_passes(o_bank[:, b - b0], b, range(G))
+            o_bank_of[b0] = o_bank
+
+        def store_out(b0, b1):
+            cols = slice(b0 * O, b1 * O)
+            nc.vector.tensor_tensor(
+                out=out_sb[:, cols],
+                in0=o_bank_of[b0][:, 0 : b1 - b0].rearrange("p b o -> p (b o)"),
+                in1=b3_all[:, cols],
+                op=ADD,
+            )
             nc.sync.dma_start(
-                out=out[:, half * HALF : (half + 1) * HALF, :].rearrange("t b o -> t (b o)"),
-                in_=out_sb[:, cols],
+                out=out[:, b0:b1, :].rearrange("t b o -> t (b o)"), in_=out_sb[:, cols]
             )
 
-        grouped_now = regroup_sw1(0)
+        regroup_sw1(0, 0, 2)
+        scalar_regroup_sw1(0)
+        regroup_sw1(0, 2, V_SLOTS)
         transpose_z2(0)
         transpose_b2()
-        quantise(sw1_codes, sw1_scales, 0, grouped_now)
-        grouped_now = regroup_sw1(1)
-        quantise_z2(0)
-        for g in range(1, G):
-            grouped_next = regroup_sw1(g + 1) if g + 1 < G else None
-            quantise(sw1_codes, sw1_scales, g * K_PASS, grouped_now)
-            grouped_now = grouped_next
-
-        for unit in range(UNITS):
-            planes = hidden_matmuls(unit)
-            if unit == 0:
-                transpose_z2(1)
-            w3_grouped = regroup_w3(unit)
-            if unit == UNITS - 1:
-                output_layer(0)
-            h_grouped = regroup_h(planes)
-            if unit == 1:
-                quantise_z2(1)
-            quantise(w3_codes, w3_scales, unit * G * O, w3_grouped)
-            quantise_h(unit, h_grouped)
-        output_layer(1)
+        transpose_z2(1)
+        quantise_sw1(0, 0, 2)
+        quantise_sw1(0, 2, 4)
+        quantise_z2(0, 2)
+        hidden_half(0, range(4), 0, 2)
+        scalar_regroup_sw1(1)
+        scalar_regroup_sw1(2)
+        regroup_sw1(1)
+        quantise_z2(2, 4)
+        hidden_half(0, range(4), 2, 4)
+        regroup_sw1(2)
+        quantise_sw1(1)
+        hidden_half(1, range(0, 2))
+        scalar_regroup_sw1(3)
+        hidden_half(1, range(2, 4))
+        spread_w3(0)
+        regroup_sw1(3)
+        quantise_sw1(2)
+        hidden_half(2)
+        regroup_half(0)
+        regroup_w3(0)
+        quantise_sw1(3)
+        quantise_half(0)
+        transpose_z2(2)
+        transpose_z2(3)
+        spread_w3(1)
+        hidden_half(3)
+        regroup_w3(1)
+        regroup_half(1)
+        quantise_w3(0)
+        quantise_half(1)
+        regroup_w3(2)
+        regroup_half(2)
+        quantise_z2(4, 8)
+        quantise_w3(1)
+        quantise_half(2)
+        spread_w3(2)
+        hidden_one(4, 0, 4)
+        regroup_w3(3)
+        regroup_half(3)
+        quantise_w3(2)
+        quantise_half(3)
+        spread_w3(3)
+        hidden_one(5, 0, 4)
+        regroup_w3(4)
+        regroup_one(4, 0, 4)
+        quantise_w3(3)
+        quantise_one(4, 0, 4)
+        spread_w3(4)
+        hidden_one(6, 0, 4)
+        spread_w3(5)
+        multiply_out(0, 4)
+        regroup_w3(5)
+        regroup_one(5, 0, 4)
+        quantise_w3(4)
+        quantise_one(5, 0, 4)
+        spread_w3(6)
+        hidden_one(7, 0, 2)
+        spread_w3(7)
+        hidden_one(7, 2, 4)
+        regroup_w3(6)
+        store_out(0, 4)
+        quantise_w3(5)
+        multiply_out(4, 6)
+        regroup_one(6, 0, 4)
+        quantise_w3(6)
+        regroup_w3(7)
+        quantise_one(6, 0, 4)
+        store_out(4, 6)
+        regroup_one(7, 0, 2)
+        quantise_w3(7)
+        quantise_one(7, 0, 2)
+        multiply_out(6, 7)
+        regroup_one(7, 2, 4)
+        store_out(6, 7)
+        quantise_one(7, 2, 4)
+        multiply_out(7, 8)
+        store_out(7, 8)

@@ -18,7 +18,7 @@ K_PASS = P * PACK
 G = H // K_PASS
 HALF = B // 2
 N_HALF = HALF * T
-V_SLOTS = 3
+V_Q = 96
 TE_G = 2
 
 S_COLS = 0
@@ -141,15 +141,19 @@ def tile_mlpmodelpredictor_pb_kernel(tc, z2, sw1, b2, w3, b3, out):
         for g in range(G):
             sw1_grouped[g] = sw1_stage.tile([P, PACK, P, PACK], BF16, name="sw1_stage", align_bytes=64)
 
-        def sw1_slots(g, j0, j1):
-            source = sw1_raw[g].rearrange("p r (q j) -> p j q r", j=PACK)
-            return {"out": sw1_grouped[g][:, j0:j1], "in_": source[:, j0:j1]}
+        def sw1_part(g, q0, q1):
+            return {
+                "out": sw1_grouped[g][:, :, q0:q1].rearrange("p j (c i) r -> p c j i r", i=2),
+                "in_": sw1_raw[g][:, :, q0 * PACK : q1 * PACK].rearrange(
+                    "p r (c i j) -> p c j i r", i=2, j=PACK
+                ),
+            }
 
-        def regroup_sw1(g, j0=0, j1=V_SLOTS):
-            nc.vector.tensor_copy(**sw1_slots(g, j0, j1))
+        def regroup_sw1(g, q0=0, q1=V_Q):
+            nc.vector.tensor_copy(**sw1_part(g, q0, q1))
 
         def scalar_regroup_sw1(g):
-            nc.scalar.copy(**sw1_slots(g, V_SLOTS, PACK))
+            nc.scalar.copy(**sw1_part(g, V_Q, P))
 
         def quantise_sw1(g, j0=0, j1=PACK):
             quantise(
@@ -303,9 +307,9 @@ def tile_mlpmodelpredictor_pb_kernel(tc, z2, sw1, b2, w3, b3, out):
                 out=out[:, b0:b1, :].rearrange("t b o -> t (b o)"), in_=out_sb[:, cols]
             )
 
-        regroup_sw1(0, 0, 2)
+        regroup_sw1(0, 0, V_Q // 2)
         scalar_regroup_sw1(0)
-        regroup_sw1(0, 2, V_SLOTS)
+        regroup_sw1(0, V_Q // 2, V_Q)
         transpose_z2(0)
         transpose_b2()
         transpose_z2(1)

@@ -21,8 +21,6 @@ N_HALF = HALF * T
 V_Q = 96
 TE_G = 2
 
-S_COLS = 0
-
 FLOPS = 2 * T * B * R * H + 2 * B * T * H * O
 
 
@@ -33,7 +31,7 @@ def tile_mlpmodelpredictor_pb_kernel(tc, z2, sw1, b2, w3, b3, out):
         sw1_in = ctx.enter_context(tc.tile_pool(name="sw1_in", bufs=G))
         w3_in = ctx.enter_context(tc.tile_pool(name="w3_in", bufs=B))
         sw1_stage = ctx.enter_context(tc.tile_pool(name="sw1_stage", bufs=G))
-        w3_stage = ctx.enter_context(tc.tile_pool(name="w3_stage", bufs=4))
+        w3_stage = ctx.enter_context(tc.tile_pool(name="w3_stage", bufs=6))
         stage = ctx.enter_context(tc.tile_pool(name="stage", bufs=3))
         plane_pool = ctx.enter_context(tc.tile_pool(name="plane_pool", bufs=6))
         banks = ctx.enter_context(tc.psum_pool(name="banks", bufs=4))
@@ -170,6 +168,12 @@ def tile_mlpmodelpredictor_pb_kernel(tc, z2, sw1, b2, w3, b3, out):
                 w3_grouped[b] = w3_stage.tile([P, G, O, PACK], BF16, name="w3_stage", align_bytes=64)
             return w3_grouped[b]
 
+        def scalar_regroup_w3(b):
+            nc.scalar.copy(
+                out=w3_stage_of(b)[:, TE_G].rearrange("p (c i) j -> p c j i", i=4),
+                in_=w3_raw[b][:, TE_G].rearrange("p j (c i) -> p c j i", i=4),
+            )
+
         def spread_w3(b):
             grouped = w3_stage_of(b)
             bank = w3_banks.tile([P, TE_G, O, PACK], BF16)
@@ -182,16 +186,11 @@ def tile_mlpmodelpredictor_pb_kernel(tc, z2, sw1, b2, w3, b3, out):
                     stop=True,
                 )
             nc.scalar.copy(out=grouped[:, 0:TE_G], in_=bank[:])
-            if S_COLS:
-                nc.scalar.copy(
-                    out=grouped[:, TE_G:G, 0:S_COLS],
-                    in_=w3_raw[b][:, TE_G:G, :, 0:S_COLS].rearrange("p g j o -> p g o j"),
-                )
 
-        def regroup_w3(b):
+        def regroup_w3(b, g0=TE_G):
             nc.vector.tensor_copy(
-                out=w3_stage_of(b)[:, TE_G:G, S_COLS:O].rearrange("p g (c i) j -> p g c j i", i=4),
-                in_=w3_raw[b][:, TE_G:G, :, S_COLS:O].rearrange("p g j (c i) -> p g c j i", i=4),
+                out=w3_stage_of(b)[:, g0:G].rearrange("p g (c i) j -> p g c j i", i=4),
+                in_=w3_raw[b][:, g0:G].rearrange("p g j (c i) -> p g c j i", i=4),
             )
 
         def quantise_w3(b):
@@ -239,7 +238,8 @@ def tile_mlpmodelpredictor_pb_kernel(tc, z2, sw1, b2, w3, b3, out):
 
         def hidden_one(b, g0, g1):
             z_cols = slice(b * T, (b + 1) * T)
-            planes = plane_pool.tile([P, g1 - g0, PACK, T], BF16, name="h_planes")
+            if b not in planes_of:
+                planes_of[b] = plane_pool.tile([P, G, PACK, T], BF16, name="h_planes")
             for g in range(g0, g1):
                 bank = banks.tile([P, PACK, T], F32, tag="bank")
                 for j in range(PACK):
@@ -254,14 +254,13 @@ def tile_mlpmodelpredictor_pb_kernel(tc, z2, sw1, b2, w3, b3, out):
                         stop=True,
                     )
                 for j in range(PACK):
-                    relu_out(planes[:, g - g0, j], bank[:, j], j, b, g)
-            planes_of[b, g0] = planes
+                    relu_out(planes_of[b][:, g, j], bank[:, j], j, b, g)
 
         def regroup_one(b, g0, g1):
             grouped = stage.tile([P, g1 - g0, T, PACK], BF16, name="h_stage", align_bytes=64)
             nc.vector.tensor_copy(
                 out=grouped.rearrange("p g (c i) j -> p g c j i", i=4),
-                in_=planes_of[b, g0].rearrange("p g j (c i) -> p g c j i", i=4),
+                in_=planes_of[b][:, g0:g1].rearrange("p g j (c i) -> p g c j i", i=4),
             )
             grouped_of[b, g0] = grouped
 
@@ -323,40 +322,41 @@ def tile_mlpmodelpredictor_pb_kernel(tc, z2, sw1, b2, w3, b3, out):
         quantise_z2(2, 4)
         hidden_half(0, range(4), 2, 4)
         regroup_sw1(2)
+        regroup_sw1(3)
         quantise_sw1(1)
         hidden_half(1, range(0, 2))
         scalar_regroup_sw1(3)
         hidden_half(1, range(2, 4))
         spread_w3(0)
-        regroup_sw1(3)
         quantise_sw1(2)
         hidden_half(2)
-        regroup_half(0)
         regroup_w3(0)
+        regroup_half(0)
+        regroup_w3(1)
         quantise_sw1(3)
         quantise_half(0)
         transpose_z2(2)
         transpose_z2(3)
         spread_w3(1)
         hidden_half(3)
-        regroup_w3(1)
+        regroup_w3(2)
         regroup_half(1)
         quantise_w3(0)
         quantise_half(1)
-        regroup_w3(2)
+        regroup_w3(3)
         regroup_half(2)
         quantise_z2(4, 8)
         quantise_w3(1)
         quantise_half(2)
         spread_w3(2)
         hidden_one(4, 0, 4)
-        regroup_w3(3)
+        regroup_w3(4)
         regroup_half(3)
         quantise_w3(2)
         quantise_half(3)
         spread_w3(3)
         hidden_one(5, 0, 4)
-        regroup_w3(4)
+        regroup_w3(5)
         regroup_one(4, 0, 4)
         quantise_w3(3)
         quantise_one(4, 0, 4)
@@ -364,29 +364,31 @@ def tile_mlpmodelpredictor_pb_kernel(tc, z2, sw1, b2, w3, b3, out):
         hidden_one(6, 0, 4)
         spread_w3(5)
         multiply_out(0, 4)
-        regroup_w3(5)
+        regroup_w3(6)
         regroup_one(5, 0, 4)
         quantise_w3(4)
         quantise_one(5, 0, 4)
         spread_w3(6)
         hidden_one(7, 0, 2)
         spread_w3(7)
+        scalar_regroup_w3(7)
         hidden_one(7, 2, 4)
-        regroup_w3(6)
+        regroup_w3(7, TE_G + 1)
         store_out(0, 4)
+        regroup_one(6, 0, 4)
         quantise_w3(5)
         multiply_out(4, 6)
-        regroup_one(6, 0, 4)
         quantise_w3(6)
-        regroup_w3(7)
         quantise_one(6, 0, 4)
-        store_out(4, 6)
         regroup_one(7, 0, 2)
+        store_out(4, 6)
         quantise_w3(7)
         quantise_one(7, 0, 2)
         multiply_out(6, 7)
-        regroup_one(7, 2, 4)
+        regroup_one(7, 2, 3)
+        regroup_one(7, 3, 4)
+        quantise_one(7, 2, 3)
+        quantise_one(7, 3, 4)
         store_out(6, 7)
-        quantise_one(7, 2, 4)
         multiply_out(7, 8)
         store_out(7, 8)

@@ -68,8 +68,6 @@ def tile_mlpmodelpredictor_pb_kernel(tc, z2, sw1, b2, w3, b3, out):
             if g == 0:
                 load_z2(0)
                 load_z2(1)
-        load_z2(2)
-        load_z2(3)
 
         w3_rows = w3.rearrange("b (g p j) o -> b p g (j o)", g=G, j=PACK)
         w3_raw = []
@@ -77,6 +75,9 @@ def tile_mlpmodelpredictor_pb_kernel(tc, z2, sw1, b2, w3, b3, out):
             raw = w3_in.tile([P, G, PACK, O], BF16, name="w3_raw")
             nc.sync.dma_start(out=raw.rearrange("p g j o -> p g (j o)"), in_=w3_rows[b])
             w3_raw.append(raw)
+            if b == 1:
+                load_z2(2)
+                load_z2(3)
 
         b3_all = keep.tile([P, B * O], BF16)
         nc.sync.dma_start(out=b3_all[:], in_=b3.rearrange("b o -> (b o)").partition_broadcast(P))
@@ -322,12 +323,12 @@ def tile_mlpmodelpredictor_pb_kernel(tc, z2, sw1, b2, w3, b3, out):
         quantise_z2(2, 4)
         hidden_half(0, range(4), 2, 4)
         regroup_sw1(2)
-        regroup_sw1(3)
         quantise_sw1(1)
         hidden_half(1, range(0, 2))
         scalar_regroup_sw1(3)
         hidden_half(1, range(2, 4))
         spread_w3(0)
+        regroup_sw1(3)
         quantise_sw1(2)
         hidden_half(2)
         regroup_w3(0)

from contextlib import ExitStack

import concourse.mybir as mybir
from concourse.masks import make_identity

BF16 = mybir.dt.bfloat16
F32 = mybir.dt.float32
U32 = mybir.dt.uint32
U8 = mybir.dt.uint8
FP8X4 = mybir.dt.float8_e4m3fn_x4
RELU = mybir.ActivationFunctionType.Relu
ADD = mybir.AluOpType.add

T, B, R, H, O = 128, 8, 512, 2048, 128
P = 128
PACK = 4
K_PASS = P * PACK
G = H // K_PASS
HALF = B // 2
N_HALF = HALF * T
V_Q = 96
TE_G = 2

FLOPS = 2 * T * B * R * H + 2 * B * T * H * O


def tile_mlpmodelpredictor_pb_kernel(tc, z2, sw1, b2, w3, b3, out):
    nc = tc.nc
    with ExitStack() as ctx:
        keep = ctx.enter_context(tc.tile_pool(name="keep", bufs=1))
        sw1_in = ctx.enter_context(tc.tile_pool(name="sw1_in", bufs=G))
        w3_in = ctx.enter_context(tc.tile_pool(name="w3_in", bufs=B))
        sw1_stage = ctx.enter_context(tc.tile_pool(name="sw1_stage", bufs=G))
        w3_stage = ctx.enter_context(tc.tile_pool(name="w3_stage", bufs=6))
        stage = ctx.enter_context(tc.tile_pool(name="stage", bufs=3))
        plane_pool = ctx.enter_context(tc.tile_pool(name="plane_pool", bufs=6))
        banks = ctx.enter_context(tc.psum_pool(name="banks", bufs=4))
        w3_banks = ctx.enter_context(tc.psum_pool(name="w3_banks", bufs=2))
        out_banks = ctx.enter_context(tc.psum_pool(name="out_banks", bufs=2))
        ctx.enter_context(tc.manual_schedule())

        b2_rows = keep.tile([P, K_PASS], BF16)
        nc.scalar.dma_start(out=b2_rows[0 : B * G, :], in_=b2.rearrange("b (g x) -> (b g) x", g=G))
        nc.vector.memset(b2_rows[32:64, :], 0.0)
        nc.vector.memset(b2_rows[64:128, :], 0.0)

        warm = keep.tile([P, 2], F32)
        nc.vector.memset(warm[:], 0.0)
        nc.scalar.activation(out=warm[:, 1:2], in_=warm[:, 0:1], func=RELU)

        z2_raw = keep.tile([P, B, R], BF16)

        def load_z2(pair):
            nc.sync.dma_start(
                out=z2_raw[:, 2 * pair : 2 * pair + 2, :], in_=z2[:, 2 * pair : 2 * pair + 2, :]
            )

        sw1_pairs = sw1.rearrange("(u q e) h -> u q e h", u=2, e=2)
        sw1_raw = []
        for g in range(G):
            raw = sw1_in.tile([P, PACK, K_PASS], BF16, name="sw1_raw")
            for u in range(2):
                nc.sync.dma_start(
                    out=raw[:, 2 * u : 2 * u + 2, :],
                    in_=sw1_pairs[u, :, :, g * K_PASS : (g + 1) * K_PASS],
                )
            sw1_raw.append(raw)
            if g == 0:
                load_z2(0)
                load_z2(1)

        w3_rows = w3.rearrange("b (g p j) o -> b p g (j o)", g=G, j=PACK)
        w3_raw = []
        for b in range(B):
            raw = w3_in.tile([P, G, PACK, O], BF16, name="w3_raw")
            nc.sync.dma_start(out=raw.rearrange("p g j o -> p g (j o)"), in_=w3_rows[b])
            w3_raw.append(raw)
            if b == 1:
                load_z2(2)
                load_z2(3)

        b3_all = keep.tile([P, B * O], BF16)
        nc.sync.dma_start(out=b3_all[:], in_=b3.rearrange("b o -> (b o)").partition_broadcast(P))

        ident = keep.tile([P, P], F32)
        make_identity(nc, ident[:])
        ident_bf = keep.tile([P, P], BF16)
        make_identity(nc, ident_bf[:])
        b2_sorted = keep.tile([P, PACK, P], F32)
        nc.vector.tensor_copy(out=b2_sorted[:], in_=b2_rows.rearrange("r (q j) -> r j q", j=PACK))
        b2_cols = keep.tile([P, PACK, B * G], F32)

        def transpose_b2():
            b2_bank = banks.tile([P, PACK, P], F32, tag="bank")
            for j in range(PACK):
                nc.tensor.transpose(b2_bank[:, j, :], b2_sorted[:, j, :], ident[:])
            nc.scalar.copy(out=b2_cols[:], in_=b2_bank[:, :, 0 : B * G])

        z_grouped = keep.tile([P, B, T, PACK], BF16, align_bytes=64)
        z_codes = keep.tile([P, B * T], U32, align_bytes=64)
        z_scales = keep.tile([P, B * T], U8, align_bytes=64)
        sw1_codes = keep.tile([P, H], U32, align_bytes=64)
        sw1_scales = keep.tile([P, H], U8, align_bytes=64)
        w3_codes = keep.tile([P, B * G * O], U32, align_bytes=64)
        w3_scales = keep.tile([P, B * G * O], U8, align_bytes=64)
        h_codes = keep.tile([P, B * G * T], U32, align_bytes=64)
        h_scales = keep.tile([P, B * G * T], U8, align_bytes=64)
        out_sb = keep.tile([P, B * O], F32)

        z2_words = z2_raw.bitcast(F32)
        z_grouped_words = z_grouped.bitcast(F32)

        def quantise(codes, scales, first, grouped):
            n = grouped.shape[1] // PACK
            nc.vector.quantize_mx(
                out=codes[:, first : first + n].bitcast(FP8X4),
                scales=scales[:, first : first + n],
                in_=grouped,
            )

        def transpose_z2(pair):
            zt = banks.tile([P, 2, 2, T], F32, tag="bank")
            for d in range(2):
                for u in range(2):
                    nc.tensor.transpose(
                        zt[:, d, u, :], z2_words[:, 2 * pair + d, u * P : (u + 1) * P], ident[:]
                    )
            nc.scalar.copy(
                out=z_grouped_words[:, 2 * pair : 2 * pair + 2, :, :],
                in_=zt.rearrange("p d u t -> p d t u"),
            )

        def quantise_z2(b0, b1):
            quantise(
                z_codes, z_scales, b0 * T, z_grouped[:, b0:b1].rearrange("p b t k -> p (b t k)")
            )

        sw1_grouped = {}

        for g in range(G):
            sw1_grouped[g] = sw1_stage.tile([P, PACK, P, PACK], BF16, name="sw1_stage", align_bytes=64)

        def sw1_part(g, q0, q1):
            return {
                "out": sw1_grouped[g][:, :, q0:q1].rearrange("p j (c i) r -> p c j i r", i=2),
                "in_": sw1_raw[g][:, :, q0 * PACK : q1 * PACK].rearrange(
                    "p r (c i j) -> p c j i r", i=2, j=PACK
                ),
            }

        def regroup_sw1(g, q0=0, q1=V_Q):
            nc.vector.tensor_copy(**sw1_part(g, q0, q1))

        def scalar_regroup_sw1(g):
            nc.scalar.copy(**sw1_part(g, V_Q, P))

        def quantise_sw1(g, j0=0, j1=PACK):
            quantise(
                sw1_codes,
                sw1_scales,
                g * K_PASS + j0 * P,
                sw1_grouped[g][:, j0:j1].rearrange("p j q r -> p (j q r)"),
            )

        w3_grouped = {}

        def w3_stage_of(b):
            if b not in w3_grouped:
                w3_grouped[b] = w3_stage.tile([P, G, O, PACK], BF16, name="w3_stage", align_bytes=64)
            return w3_grouped[b]

        def scalar_regroup_w3(b):
            nc.scalar.copy(
                out=w3_stage_of(b)[:, TE_G].rearrange("p (c i) j -> p c j i", i=4),
                in_=w3_raw[b][:, TE_G].rearrange("p j (c i) -> p c j i", i=4),
            )

        def spread_w3(b):
            grouped = w3_stage_of(b)
            bank = w3_banks.tile([P, TE_G, O, PACK], BF16)
            for g in range(TE_G):
                nc.tensor.matmul(
                    bank[:, g],
                    lhsT=ident_bf[:],
                    rhs=w3_raw[b][:, g].rearrange("p j o -> p o j"),
                    start=True,
                    stop=True,
                )
            nc.scalar.copy(out=grouped[:, 0:TE_G], in_=bank[:])

        def regroup_w3(b, g0=TE_G):
            nc.vector.tensor_copy(
                out=w3_stage_of(b)[:, g0:G].rearrange("p g (c i) j -> p g c j i", i=4),
                in_=w3_raw[b][:, g0:G].rearrange("p g j (c i) -> p g c j i", i=4),
            )

        def quantise_w3(b):
            quantise(
                w3_codes, w3_scales, b * G * O, w3_grouped[b].rearrange("p g o j -> p (g o j)")
            )

        planes_of = {}
        grouped_of = {}

        def relu_out(plane, bank, j, b, g):
            nc.scalar.activation(
                out=plane, in_=bank, func=RELU, bias=b2_cols[:, j, b * G + g : b * G + g + 1], scale=1.0
            )

        def hidden_half(g, slots=range(PACK), b0=0, b1=HALF):
            if ("half", g) not in planes_of:
                planes_of["half", g] = plane_pool.tile([P, PACK, N_HALF], BF16, name="h_planes")
            planes = planes_of["half", g]
            for j in slots:
                w_cols = slice((g * PACK + j) * P, (g * PACK + j + 1) * P)
                bank = banks.tile([P, HALF, T], F32, tag="bank")
                nc.tensor.matmul_mx(
                    out=bank[:, 0 : b1 - b0].rearrange("p b t -> p (b t)"),
                    lhsT=sw1_codes[:, w_cols].bitcast(FP8X4),
                    lhsT_scale=sw1_scales[:, w_cols],
                    rhs=z_codes[:, b0 * T : b1 * T].bitcast(FP8X4),
                    rhs_scale=z_scales[:, b0 * T : b1 * T],
                    start=True,
                    stop=True,
                )
                for b in range(b0, b1):
                    relu_out(planes[:, j, b * T : (b + 1) * T], bank[:, b - b0], j, b, g)

        def regroup_half(g):
            grouped = stage.tile([P, N_HALF, PACK], BF16, name="h_stage", align_bytes=64)
            nc.vector.tensor_copy(
                out=grouped.rearrange("p (c i) j -> p c j i", i=4),
                in_=planes_of["half", g].rearrange("p j (c i) -> p c j i", i=4),
            )
            grouped_of["half", g] = grouped

        def quantise_half(g):
            quantise(h_codes, h_scales, g * N_HALF, grouped_of["half", g].rearrange("p n j -> p (n j)"))

        def hidden_one(b, g0, g1):
            z_cols = slice(b * T, (b + 1) * T)
            if b not in planes_of:
                planes_of[b] = plane_pool.tile([P, G, PACK, T], BF16, name="h_planes")
            for g in range(g0, g1):
                bank = banks.tile([P, PACK, T], F32, tag="bank")
                for j in range(PACK):
                    w_cols = slice((g * PACK + j) * P, (g * PACK + j + 1) * P)
                    nc.tensor.matmul_mx(
                        out=bank[:, j],
                        lhsT=sw1_codes[:, w_cols].bitcast(FP8X4),
                        lhsT_scale=sw1_scales[:, w_cols],
                        rhs=z_codes[:, z_cols].bitcast(FP8X4),
                        rhs_scale=z_scales[:, z_cols],
                        start=True,
                        stop=True,
                    )
                for j in range(PACK):
                    relu_out(planes_of[b][:, g, j], bank[:, j], j, b, g)

        def regroup_one(b, g0, g1):
            grouped = stage.tile([P, g1 - g0, T, PACK], BF16, name="h_stage", align_bytes=64)
            nc.vector.tensor_copy(
                out=grouped.rearrange("p g (c i) j -> p g c j i", i=4),
                in_=planes_of[b][:, g0:g1].rearrange("p g j (c i) -> p g c j i", i=4),
            )
            grouped_of[b, g0] = grouped

        def quantise_one(b, g0, g1):
            quantise(
                h_codes,
                h_scales,
                (b * G + g0) * T,
                grouped_of[b, g0].rearrange("p g n j -> p (g n j)"),
            )

        def output_passes(o_out, b, gs):
            for g in gs:
                h_first = g * N_HALF + b * T if b < HALF else (b * G + g) * T
                w_first = (b * G + g) * O
                nc.tensor.matmul_mx(
                    out=o_out,
                    lhsT=h_codes[:, h_first : h_first + T].bitcast(FP8X4),
                    lhsT_scale=h_scales[:, h_first : h_first + T],
                    rhs=w3_codes[:, w_first : w_first + O].bitcast(FP8X4),
                    rhs_scale=w3_scales[:, w_first : w_first + O],
                    start=(g == 0),
                    stop=(g == G - 1),
                )

        o_bank_of = {}

        def multiply_out(b0, b1):
            o_bank = out_banks.tile([P, HALF, O], F32, name="o_bank")
            for b in range(b0, b1):
                output_passes(o_bank[:, b - b0], b, range(G))
            o_bank_of[b0] = o_bank

        def store_out(b0, b1):
            cols = slice(b0 * O, b1 * O)
            nc.vector.tensor_tensor(
                out=out_sb[:, cols],
                in0=o_bank_of[b0][:, 0 : b1 - b0].rearrange("p b o -> p (b o)"),
                in1=b3_all[:, cols],
                op=ADD,
            )
            nc.sync.dma_start(
                out=out[:, b0:b1, :].rearrange("t b o -> t (b o)"), in_=out_sb[:, cols]
            )

        regroup_sw1(0, 0, V_Q // 2)
        scalar_regroup_sw1(0)
        regroup_sw1(0, V_Q // 2, V_Q)
        transpose_z2(0)
        transpose_b2()
        transpose_z2(1)
        quantise_sw1(0, 0, 2)
        quantise_sw1(0, 2, 4)
        quantise_z2(0, 2)
        hidden_half(0, range(4), 0, 2)
        scalar_regroup_sw1(1)
        scalar_regroup_sw1(2)
        regroup_sw1(1)
        quantise_z2(2, 4)
        hidden_half(0, range(4), 2, 4)
        regroup_sw1(2)
        quantise_sw1(1)
        hidden_half(1, range(0, 2))
        scalar_regroup_sw1(3)
        hidden_half(1, range(2, 4))
        spread_w3(0)
        regroup_sw1(3)
        quantise_sw1(2)
        hidden_half(2)
        regroup_w3(0)
        regroup_half(0)
        regroup_w3(1)
        quantise_sw1(3)
        quantise_half(0)
        transpose_z2(2)
        transpose_z2(3)
        spread_w3(1)
        hidden_half(3)
        regroup_w3(2)
        regroup_half(1)
        quantise_w3(0)
        quantise_half(1)
        regroup_w3(3)
        regroup_half(2)
        quantise_z2(4, 8)
        quantise_w3(1)
        quantise_half(2)
        spread_w3(2)
        hidden_one(4, 0, 4)
        regroup_w3(4)
        regroup_half(3)
        quantise_w3(2)
        quantise_half(3)
        spread_w3(3)
        hidden_one(5, 0, 4)
        regroup_w3(5)
        regroup_one(4, 0, 4)
        quantise_w3(3)
        quantise_one(4, 0, 4)
        spread_w3(4)
        hidden_one(6, 0, 4)
        spread_w3(5)
        multiply_out(0, 4)
        regroup_w3(6)
        regroup_one(5, 0, 4)
        quantise_w3(4)
        quantise_one(5, 0, 4)
        spread_w3(6)
        hidden_one(7, 0, 2)
        spread_w3(7)
        scalar_regroup_w3(7)
        hidden_one(7, 2, 4)
        regroup_w3(7, TE_G + 1)
        store_out(0, 4)
        regroup_one(6, 0, 4)
        quantise_w3(5)
        multiply_out(4, 6)
        quantise_w3(6)
        quantise_one(6, 0, 4)
        regroup_one(7, 0, 2)
        store_out(4, 6)
        quantise_w3(7)
        quantise_one(7, 0, 2)
        multiply_out(6, 7)
        regroup_one(7, 2, 3)
        regroup_one(7, 3, 4)
        quantise_one(7, 2, 3)
        quantise_one(7, 3, 4)
        store_out(6, 7)
        multiply_out(7, 8)
        store_out(7, 8)
